import numpy as np
import ml_dtypes


def mxq(x, axis, fmt="e4m3"):
    dtype, down = {"e4m3": (ml_dtypes.float8_e4m3fn, 7), "e5m2": (ml_dtypes.float8_e5m2, 14)}[fmt]
    v = np.moveaxis(np.asarray(x, np.float32).astype(ml_dtypes.bfloat16).astype(np.float64), axis, -1)
    blocks = v.reshape(v.shape[:-1] + (-1, 32))
    amax = np.abs(blocks).max(-1, keepdims=True)
    byte = np.maximum(np.where(amax > 0, np.frexp(amax)[1] - 1 + 127, 0) - down, 1)
    scale = np.exp2(byte - 127.0)
    codes = (blocks / scale).astype(np.float32).astype(dtype).astype(np.float64)
    return np.moveaxis((codes * scale).reshape(v.shape), -1, axis)


WIDE = False


def mx_kscale(k):
    if not WIDE:
        return np.ones(k)
    levels = np.array([10, -10, 5, -5, 0])
    a = np.random.permutation(np.resize(levels, k // 512 * 4)).reshape(k // 512, 4)
    idx = np.arange(k)
    return np.exp2(a[idx // 512, idx % 128 // 32])


BF16 = ml_dtypes.bfloat16


def bf(x):
    return np.asarray(x, np.float32).astype(BF16)


def f64(x):
    return np.asarray(x).astype(np.float64)


B, S, D, DFF, R = 4, 2048, 512, 1024, 512


def setup_inputs():
    t, r = mx_kscale(DFF), mx_kscale(R)
    v = np.random.standard_normal((B, S, DFF)) * 1.2
    return {"h_gelu": bf(v / (1.0 + np.exp(-1.702 * v)) * t),
            "c_proj_U": bf(np.random.standard_normal((DFF, R)) * 2.0 / np.sqrt(DFF) / t[:, None]),
            "c_proj_S": bf(np.random.uniform(size=R) * r),
            "c_proj_V": bf(np.random.standard_normal((D, R)) / np.sqrt(R) / r[None, :]),
            "c_proj_bias": bf(np.random.standard_normal(D) * 0.3)}


def reference(h_gelu, c_proj_U, c_proj_S, c_proj_V, c_proj_bias):
    us = f64(c_proj_U) * f64(c_proj_S)[None, :]
    w = mxq(us, 1, "e4m3") @ mxq(f64(c_proj_V), 1, "e4m3").T
    return (mxq(f64(h_gelu), 2, "e4m3") @ mxq(w, 0, "e4m3")) + f64(c_proj_bias)

@@ -1,0 +1,245 @@
+from contextlib import ExitStack
+
+import concourse.mybir as mybir
+from concourse.masks import make_identity
+
+F32 = mybir.dt.float32
+BF16 = mybir.dt.bfloat16
+U32 = mybir.dt.uint32
+U8 = mybir.dt.uint8
+FP8X4 = mybir.dt.float8_e4m3fn_x4
+MULT = mybir.AluOpType.mult
+ADD = mybir.AluOpType.add
+
+P = 128
+PACK = 4
+TOKENS = 4 * 2048
+DFF = 1024
+R = 512
+D = 512
+
+BANK = 512
+PLANES = DFF // P
+PASSES = DFF // (P * PACK)
+TILES = 4
+CHUNK = TILES * P
+N_CHUNKS = TOKENS // CHUNK
+
+LOOKAHEAD = 2
+H_BUFS = 8
+
+FLOPS = 2 * DFF * R * D + 2 * TOKENS * DFF * D
+
+
+def tile_hybridsuperlayer_pb_t_kernel(
+    tc, h_gelu, c_proj_U, c_proj_S, c_proj_V, c_proj_bias, out
+):
+    nc = tc.nc
+    h_chunks = h_gelu.flatten_outer_dims().rearrange("(c p i) k -> c p (i k)", p=P, i=TILES)
+    out_chunks = out.flatten_outer_dims().rearrange("(c p i) d -> c p (i d)", p=P, i=TILES)
+
+    with ExitStack() as ctx:
+        ctx.enter_context(tc.manual_schedule())
+        const = ctx.enter_context(tc.tile_pool(name="const", bufs=1))
+        weights = ctx.enter_context(tc.tile_pool(name="weights", bufs=1))
+        h_pool = ctx.enter_context(tc.tile_pool(name="h", bufs=H_BUFS))
+        grouped_pool = ctx.enter_context(tc.tile_pool(name="grouped", bufs=3))
+        codes_pool = ctx.enter_context(tc.tile_pool(name="codes", bufs=LOOKAHEAD + 2))
+        out_pool = ctx.enter_context(tc.tile_pool(name="outs", bufs=4))
+        xt_pool = ctx.enter_context(tc.psum_pool(name="xt", bufs=4))
+        acc_pool = ctx.enter_context(tc.psum_pool(name="acc", bufs=4))
+
+        ident = const.tile([P, P], F32)
+        make_identity(nc, ident[:])
+        ones = const.tile([P, P], BF16)
+        nc.vector.memset(ones[:], 1.0)
+        bias_rows = const.tile([P, D], BF16)
+        nc.vector.memset(bias_rows[:], 0.0)
+
+        s_quad = const.tile([P, PACK], BF16)
+        with nc.allow_non_contiguous_dma(reason="512 singular values, two to a piece"):
+            nc.scalar.dma_start(
+                out=s_quad[:].rearrange("q (a b) -> q a b", b=2),
+                in_=c_proj_S.rearrange("(a q b) -> q a b", a=2, b=2),
+            )
+        nc.scalar.dma_start(out=bias_rows[0:1, :], in_=c_proj_bias.rearrange("(o d) -> o d", o=1))
+
+        u_sb = weights.tile([P, PLANES * R], BF16)
+        u_view = u_sb[:].rearrange("p (c x) -> p c x", c=4)
+        u_dram = c_proj_U.rearrange("(c p e) r -> p c (e r)", c=4, e=2)
+        for first in (0, 2):
+            nc.sync.dma_start(out=u_view[:, first : first + 2, :], in_=u_dram[:, first : first + 2, :])
+        v_sb = weights.tile([P, (D // P) * R], BF16)
+        nc.sync.dma_start(
+            out=v_sb[:].rearrange("p (t r) -> p t r", r=R),
+            in_=c_proj_V.rearrange("(t p) r -> p t r", p=P),
+        )
+
+        h_tiles = {}
+
+        def load_chunk(c):
+            h_sb = h_pool.tile([P, TILES * DFF], BF16)
+            nc.sync.dma_start(out=h_sb[:], in_=h_chunks[c])
+            h_tiles[c] = h_sb
+
+        for c in range(H_BUFS):
+            load_chunk(c)
+
+        bias_ps = acc_pool.tile([P, D], F32, tag="acc")
+        nc.tensor.matmul(out=bias_ps[:], lhsT=ones[:], rhs=bias_rows[:], start=True, stop=True)
+        bias_bc = const.tile([P, D], F32)
+        nc.scalar.copy(out=bias_bc[:], in_=bias_ps[:])
+
+        u_words = u_sb[:].bitcast(F32)
+        us_grouped = weights.tile([P, PLANES * P * PACK], BF16, align_bytes=64)
+        s_repeated = (
+            s_quad[:].rearrange("q (a b) -> q a b", b=2).unsqueeze(1).to_broadcast([P, P, 2, 2])
+        )
+        for c in range(PLANES // 2):
+            ut = xt_pool.tile([P, BANK], F32, tag="xt")
+            for e in range(2):
+                for a in range(2):
+                    nc.tensor.transpose(
+                        ut[:, (2 * e + a) * P : (2 * e + a + 1) * P],
+                        u_words[:, (4 * c + 2 * e + a) * P : (4 * c + 2 * e + a + 1) * P],
+                        ident[:],
+                    )
+            ut_pairs = ut[:].bitcast(BF16).rearrange("q (e a m b) -> q e m a b", e=2, a=2, b=2)
+            for e in range(2):
+                j = 2 * c + e
+                nc.vector.tensor_tensor(
+                    out=us_grouped[:, j * P * PACK : (j + 1) * P * PACK].rearrange(
+                        "q (m a b) -> q m a b", a=2, b=2
+                    ),
+                    in0=ut_pairs[:, e],
+                    in1=s_repeated,
+                    op=MULT,
+                )
+
+        v_words = v_sb[:].bitcast(F32)
+        v_grouped = weights.tile([P, D * PACK], BF16, align_bytes=64)
+        v_grouped_words = v_grouped[:].bitcast(F32).rearrange("q (d a) -> q d a", a=2)
+        for half in range(2):
+            vt = xt_pool.tile([P, BANK], F32, tag="xt")
+            for a in range(2):
+                for s in range(2):
+                    t = 2 * half + s
+                    nc.tensor.transpose(
+                        vt[:, (2 * a + s) * P : (2 * a + s + 1) * P],
+                        v_words[:, (2 * t + a) * P : (2 * t + a + 1) * P],
+                        ident[:],
+                    )
+            nc.scalar.copy(
+                out=v_grouped_words[:, half * 256 : (half + 1) * 256, :],
+                in_=vt[:].rearrange("q (a d) -> q d a", a=2),
+            )
+
+        v_codes = weights.tile([P, D], U32, align_bytes=64)
+        v_scales = weights.tile([P, D], U8, align_bytes=64)
+        nc.vector.quantize_mx(out=v_codes[:].bitcast(FP8X4), scales=v_scales[:], in_=v_grouped[:])
+        us_codes = weights.tile([P, PLANES * P], U32, align_bytes=64)
+        us_scales = weights.tile([P, PLANES * P], U8, align_bytes=64)
+        nc.vector.quantize_mx(
+            out=us_codes[:].bitcast(FP8X4), scales=us_scales[:], in_=us_grouped[:]
+        )
+
+        grouped_tiles = {}
+        code_tiles = {}
+
+        def transpose_chunk(c):
+            h_words = h_tiles[c][:].bitcast(F32)
+            grouped = grouped_pool.tile([P, CHUNK * PASSES * PACK], BF16, align_bytes=64)
+            grouped_words = grouped[:].bitcast(F32).rearrange(
+                "q (i g m u) -> q i g m u", i=TILES, g=PASSES, u=2
+            )
+            for i in range(TILES):
+                xt = xt_pool.tile([P, BANK], F32, tag="xt")
+                for w in range(BANK // P):
+                    nc.tensor.transpose(
+                        xt[:, w * P : (w + 1) * P],
+                        h_words[:, (4 * i + w) * P : (4 * i + w + 1) * P],
+                        ident[:],
+                    )
+                nc.scalar.copy(
+                    out=grouped_words[:, i],
+                    in_=xt[:].rearrange("q (g u m) -> q g m u", g=PASSES, u=2),
+                )
+            grouped_tiles[c] = grouped
+            if c + H_BUFS < N_CHUNKS:
+                load_chunk(c + H_BUFS)
+
+        def quantise_chunk(c):
+            h_codes = codes_pool.tile([P, CHUNK * PASSES], U32, align_bytes=64)
+            h_scales = codes_pool.tile([P, CHUNK * PASSES], U8, align_bytes=64)
+            nc.vector.quantize_mx(
+                out=h_codes[:].bitcast(FP8X4), scales=h_scales[:], in_=grouped_tiles[c][:]
+            )
+            code_tiles[c] = (h_codes, h_scales)
+
+        def multiply_chunk(c):
+            h_codes, h_scales = code_tiles[c]
+            out_sb = out_pool.tile([P, TILES * D], F32)
+            for i in range(TILES):
+                acc = acc_pool.tile([P, D], F32, tag="acc")
+                for g in range(PASSES):
+                    tokens = slice((PASSES * i + g) * P, (PASSES * i + g + 1) * P)
+                    features = slice(g * D, (g + 1) * D)
+                    nc.tensor.matmul_mx(
+                        out=acc[:],
+                        lhsT=h_codes[:, tokens].bitcast(FP8X4),
+                        lhsT_scale=h_scales[:, tokens],
+                        rhs=w_codes[:, features].bitcast(FP8X4),
+                        rhs_scale=w_scales[:, features],
+                        start=(g == 0),
+                        stop=(g == PASSES - 1),
+                    )
+                nc.vector.tensor_tensor(
+                    out=out_sb[:, i * D : (i + 1) * D], in0=acc[:], in1=bias_bc[:], op=ADD
+                )
+            nc.sync.dma_start(out=out_chunks[c], in_=out_sb[:])
+
+        transpose_chunk(0)
+
+        w_planes = weights.tile([P, PLANES * D], BF16)
+        for j in range(PLANES):
+            w_ps = acc_pool.tile([P, D], F32, tag="acc")
+            nc.tensor.matmul_mx(
+                out=w_ps[:],
+                lhsT=us_codes[:, j * P : (j + 1) * P].bitcast(FP8X4),
+                lhsT_scale=us_scales[:, j * P : (j + 1) * P],
+                rhs=v_codes[:].bitcast(FP8X4),
+                rhs_scale=v_scales[:],
+                start=True,
+                stop=True,
+            )
+            nc.scalar.copy(out=w_planes[:, j * D : (j + 1) * D], in_=w_ps[:])
+
+        quantise_chunk(0)
+
+        w_grouped = weights.tile([P, PASSES * D * PACK], BF16, align_bytes=64)
+        pass_cols = D * PACK
+        for g in range(PASSES):
+            nc.vector.tensor_copy(
+                out=w_grouped[:, g * pass_cols : (g + 1) * pass_cols].rearrange(
+                    "p (c i t) -> p c t i", i=4, t=PACK
+                ),
+                in_=w_planes[:, g * pass_cols : (g + 1) * pass_cols].rearrange(
+                    "p (t c i) -> p c t i", t=PACK, i=4
+                ),
+            )
+        w_codes = weights.tile([P, PASSES * D], U32, align_bytes=64)
+        w_scales = weights.tile([P, PASSES * D], U8, align_bytes=64)
+        nc.vector.quantize_mx(out=w_codes[:].bitcast(FP8X4), scales=w_scales[:], in_=w_grouped[:])
+
+        for c in range(1, LOOKAHEAD):
+            transpose_chunk(c)
+        for c in range(1, LOOKAHEAD - 1):
+            quantise_chunk(c)
+
+        for c in range(N_CHUNKS):
+            ahead = c + LOOKAHEAD
+            if ahead < N_CHUNKS:
+                transpose_chunk(ahead)
+            if 0 < ahead - 1 < N_CHUNKS:
+                quantise_chunk(ahead - 1)
+            multiply_chunk(c)

@@ -58,22 +58,22 @@ def tile_hybridsuperlayer_pb_t_kernel(
 
         s_quad = const.tile([P, PACK], BF16)
         with nc.allow_non_contiguous_dma(reason="512 singular values, two to a piece"):
-            nc.scalar.dma_start(
+            nc.sync.dma_start(
                 out=s_quad[:].rearrange("q (a b) -> q a b", b=2),
                 in_=c_proj_S.rearrange("(a q b) -> q a b", a=2, b=2),
             )
-        nc.scalar.dma_start(out=bias_rows[0:1, :], in_=c_proj_bias.rearrange("(o d) -> o d", o=1))
 
         u_sb = weights.tile([P, PLANES * R], BF16)
         u_view = u_sb[:].rearrange("p (c x) -> p c x", c=4)
         u_dram = c_proj_U.rearrange("(c p e) r -> p c (e r)", c=4, e=2)
-        for first in (0, 2):
-            nc.sync.dma_start(out=u_view[:, first : first + 2, :], in_=u_dram[:, first : first + 2, :])
+        for c in range(4):
+            nc.sync.dma_start(out=u_view[:, c, :], in_=u_dram[:, c, :])
         v_sb = weights.tile([P, (D // P) * R], BF16)
         nc.sync.dma_start(
             out=v_sb[:].rearrange("p (t r) -> p t r", r=R),
             in_=c_proj_V.rearrange("(t p) r -> p t r", p=P),
         )
+        nc.sync.dma_start(out=bias_rows[0:1, :], in_=c_proj_bias.rearrange("(o d) -> o d", o=1))
 
         h_tiles = {}
 
@@ -84,11 +84,6 @@ def tile_hybridsuperlayer_pb_t_kernel(
 
         for c in range(H_BUFS):
             load_chunk(c)
-
-        bias_ps = acc_pool.tile([P, D], F32, tag="acc")
-        nc.tensor.matmul(out=bias_ps[:], lhsT=ones[:], rhs=bias_rows[:], start=True, stop=True)
-        bias_bc = const.tile([P, D], F32)
-        nc.scalar.copy(out=bias_bc[:], in_=bias_ps[:])
 
         u_words = u_sb[:].bitcast(F32)
         us_grouped = weights.tile([P, PLANES * P * PACK], BF16, align_bytes=64)
@@ -139,9 +134,12 @@ def tile_hybridsuperlayer_pb_t_kernel(
         nc.vector.quantize_mx(out=v_codes[:].bitcast(FP8X4), scales=v_scales[:], in_=v_grouped[:])
         us_codes = weights.tile([P, PLANES * P], U32, align_bytes=64)
         us_scales = weights.tile([P, PLANES * P], U8, align_bytes=64)
-        nc.vector.quantize_mx(
-            out=us_codes[:].bitcast(FP8X4), scales=us_scales[:], in_=us_grouped[:]
-        )
+        for g in range(PASSES):
+            nc.vector.quantize_mx(
+                out=us_codes[:, g * PACK * P : (g + 1) * PACK * P].bitcast(FP8X4),
+                scales=us_scales[:, g * PACK * P : (g + 1) * PACK * P],
+                in_=us_grouped[:, g * PACK * P * PACK : (g + 1) * PACK * P * PACK],
+            )
 
         grouped_tiles = {}
         code_tiles = {}
@@ -200,33 +198,36 @@ def tile_hybridsuperlayer_pb_t_kernel(
 
         transpose_chunk(0)
 
-        w_planes = weights.tile([P, PLANES * D], BF16)
-        for j in range(PLANES):
-            w_ps = acc_pool.tile([P, D], F32, tag="acc")
-            nc.tensor.matmul_mx(
-                out=w_ps[:],
-                lhsT=us_codes[:, j * P : (j + 1) * P].bitcast(FP8X4),
-                lhsT_scale=us_scales[:, j * P : (j + 1) * P],
-                rhs=v_codes[:].bitcast(FP8X4),
-                rhs_scale=v_scales[:],
-                start=True,
-                stop=True,
-            )
-            nc.scalar.copy(out=w_planes[:, j * D : (j + 1) * D], in_=w_ps[:])
+        bias_ps = acc_pool.tile([P, D], F32, tag="acc")
+        nc.tensor.matmul(out=bias_ps[:], lhsT=ones[:], rhs=bias_rows[:], start=True, stop=True)
+        bias_bc = const.tile([P, D], F32)
+        nc.scalar.copy(out=bias_bc[:], in_=bias_ps[:])
+
+        w_grouped = weights.tile([P, PASSES * D * PACK], BF16, align_bytes=64)
+        for g in range(PASSES):
+            for block in range(D // P):
+                w_ps = acc_pool.tile([P, BANK], F32, tag="acc")
+                for t in range(PACK):
+                    j = PACK * g + t
+                    nc.tensor.matmul_mx(
+                        out=w_ps[:, t * P : (t + 1) * P],
+                        lhsT=us_codes[:, j * P : (j + 1) * P].bitcast(FP8X4),
+                        lhsT_scale=us_scales[:, j * P : (j + 1) * P],
+                        rhs=v_codes[:, block * P : (block + 1) * P].bitcast(FP8X4),
+                        rhs_scale=v_scales[:, block * P : (block + 1) * P],
+                        start=True,
+                        stop=True,
+                    )
+                first = (g * (D // P) + block) * BANK
+                words_out = w_grouped[:, first : first + BANK].rearrange("p (d t) -> p d t", t=PACK)
+                planes_in = w_ps[:].rearrange("p (t d) -> p d t", t=PACK)
+                if block % 2 == 0:
+                    nc.scalar.copy(out=words_out, in_=planes_in)
+                else:
+                    nc.vector.tensor_copy(out=words_out, in_=planes_in)
 
         quantise_chunk(0)
 
-        w_grouped = weights.tile([P, PASSES * D * PACK], BF16, align_bytes=64)
-        pass_cols = D * PACK
-        for g in range(PASSES):
-            nc.vector.tensor_copy(
-                out=w_grouped[:, g * pass_cols : (g + 1) * pass_cols].rearrange(
-                    "p (c i t) -> p c t i", i=4, t=PACK
-                ),
-                in_=w_planes[:, g * pass_cols : (g + 1) * pass_cols].rearrange(
-                    "p (t c i) -> p c t i", t=PACK, i=4
-                ),
-            )
         w_codes = weights.tile([P, PASSES * D], U32, align_bytes=64)
         w_scales = weights.tile([P, PASSES * D], U8, align_bytes=64)
         nc.vector.quantize_mx(out=w_codes[:].bitcast(FP8X4), scales=w_scales[:], in_=w_grouped[:])

@@ -25,7 +25,7 @@ TILES = 4
 CHUNK = TILES * P
 N_CHUNKS = TOKENS // CHUNK
 
-LOOKAHEAD = 2
+RUN = 2
 H_BUFS = 8
 
 FLOPS = 2 * DFF * R * D + 2 * TOKENS * DFF * D
@@ -44,8 +44,8 @@ def tile_hybridsuperlayer_pb_t_kernel(
         weights = ctx.enter_context(tc.tile_pool(name="weights", bufs=1))
         h_pool = ctx.enter_context(tc.tile_pool(name="h", bufs=H_BUFS))
         grouped_pool = ctx.enter_context(tc.tile_pool(name="grouped", bufs=3))
-        codes_pool = ctx.enter_context(tc.tile_pool(name="codes", bufs=LOOKAHEAD + 2))
-        out_pool = ctx.enter_context(tc.tile_pool(name="outs", bufs=4))
+        codes_pool = ctx.enter_context(tc.tile_pool(name="codes", bufs=2 * RUN))
+        out_pool = ctx.enter_context(tc.tile_pool(name="outs", bufs=6))
         xt_pool = ctx.enter_context(tc.psum_pool(name="xt", bufs=4))
         acc_pool = ctx.enter_context(tc.psum_pool(name="acc", bufs=4))
 
@@ -88,28 +88,26 @@ def tile_hybridsuperlayer_pb_t_kernel(
         u_words = u_sb[:].bitcast(F32)
         us_grouped = weights.tile([P, PLANES * P * PACK], BF16, align_bytes=64)
         s_repeated = (
-            s_quad[:].rearrange("q (a b) -> q a b", b=2).unsqueeze(1).to_broadcast([P, P, 2, 2])
+            s_quad[:].rearrange("q (a b) -> q a b", b=2).unsqueeze(1).to_broadcast([P, 2 * P, 2, 2])
         )
+        pair_cols = 2 * P * PACK
         for c in range(PLANES // 2):
             ut = xt_pool.tile([P, BANK], F32, tag="xt")
             for e in range(2):
                 for a in range(2):
                     nc.tensor.transpose(
-                        ut[:, (2 * e + a) * P : (2 * e + a + 1) * P],
+                        ut[:, (2 * a + e) * P : (2 * a + e + 1) * P],
                         u_words[:, (4 * c + 2 * e + a) * P : (4 * c + 2 * e + a + 1) * P],
                         ident[:],
                     )
-            ut_pairs = ut[:].bitcast(BF16).rearrange("q (e a m b) -> q e m a b", e=2, a=2, b=2)
-            for e in range(2):
-                j = 2 * c + e
-                nc.vector.tensor_tensor(
-                    out=us_grouped[:, j * P * PACK : (j + 1) * P * PACK].rearrange(
-                        "q (m a b) -> q m a b", a=2, b=2
-                    ),
-                    in0=ut_pairs[:, e],
-                    in1=s_repeated,
-                    op=MULT,
-                )
+            nc.vector.tensor_tensor(
+                out=us_grouped[:, c * pair_cols : (c + 1) * pair_cols].rearrange(
+                    "q (n a b) -> q n a b", a=2, b=2
+                ),
+                in0=ut[:].bitcast(BF16).rearrange("q (a n b) -> q n a b", a=2, b=2),
+                in1=s_repeated,
+                op=MULT,
+            )
 
         v_words = v_sb[:].bitcast(F32)
         v_grouped = weights.tile([P, D * PACK], BF16, align_bytes=64)
@@ -181,20 +179,22 @@ def tile_hybridsuperlayer_pb_t_kernel(
                 acc = acc_pool.tile([P, D], F32, tag="acc")
                 for g in range(PASSES):
                     tokens = slice((PASSES * i + g) * P, (PASSES * i + g + 1) * P)
-                    features = slice(g * D, (g + 1) * D)
+                    w_cols = slice(g * D, (g + 1) * D)
                     nc.tensor.matmul_mx(
                         out=acc[:],
                         lhsT=h_codes[:, tokens].bitcast(FP8X4),
                         lhsT_scale=h_scales[:, tokens],
-                        rhs=w_codes[:, features].bitcast(FP8X4),
-                        rhs_scale=w_scales[:, features],
+                        rhs=w_codes[:, w_cols].bitcast(FP8X4),
+                        rhs_scale=w_scales[:, w_cols],
                         start=(g == 0),
                         stop=(g == PASSES - 1),
                     )
-                nc.vector.tensor_tensor(
-                    out=out_sb[:, i * D : (i + 1) * D], in0=acc[:], in1=bias_bc[:], op=ADD
-                )
-            nc.sync.dma_start(out=out_chunks[c], in_=out_sb[:])
+                tile_cols = slice(i * D, (i + 1) * D)
+                nc.vector.tensor_tensor(out=out_sb[:, tile_cols], in0=acc[:], in1=bias_bc[:], op=ADD)
+                if c == N_CHUNKS - 1:
+                    nc.sync.dma_start(out=out_chunks[c][:, tile_cols], in_=out_sb[:, tile_cols])
+            if c < N_CHUNKS - 1:
+                nc.sync.dma_start(out=out_chunks[c], in_=out_sb[:])
 
         transpose_chunk(0)
 
@@ -232,15 +232,14 @@ def tile_hybridsuperlayer_pb_t_kernel(
         w_scales = weights.tile([P, PASSES * D], U8, align_bytes=64)
         nc.vector.quantize_mx(out=w_codes[:].bitcast(FP8X4), scales=w_scales[:], in_=w_grouped[:])
 
-        for c in range(1, LOOKAHEAD):
+        for c in range(1, RUN):
             transpose_chunk(c)
-        for c in range(1, LOOKAHEAD - 1):
             quantise_chunk(c)
 
-        for c in range(N_CHUNKS):
-            ahead = c + LOOKAHEAD
-            if ahead < N_CHUNKS:
-                transpose_chunk(ahead)
-            if 0 < ahead - 1 < N_CHUNKS:
-                quantise_chunk(ahead - 1)
-            multiply_chunk(c)
+        for first in range(0, N_CHUNKS, RUN):
+            for c in range(first + RUN, min(first + 2 * RUN, N_CHUNKS)):
+                transpose_chunk(c)
+            for c in range(first, first + RUN):
+                multiply_chunk(c)
+                if c + RUN < N_CHUNKS:
+                    quantise_chunk(c + RUN)

@@ -25,8 +25,9 @@ TILES = 4
 CHUNK = TILES * P
 N_CHUNKS = TOKENS // CHUNK
 
-RUN = 2
+LOOKAHEAD = 2
 H_BUFS = 8
+OUT_BUFS = 8
 
 FLOPS = 2 * DFF * R * D + 2 * TOKENS * DFF * D
 
@@ -44,8 +45,8 @@ def tile_hybridsuperlayer_pb_t_kernel(
         weights = ctx.enter_context(tc.tile_pool(name="weights", bufs=1))
         h_pool = ctx.enter_context(tc.tile_pool(name="h", bufs=H_BUFS))
         grouped_pool = ctx.enter_context(tc.tile_pool(name="grouped", bufs=3))
-        codes_pool = ctx.enter_context(tc.tile_pool(name="codes", bufs=2 * RUN))
-        out_pool = ctx.enter_context(tc.tile_pool(name="outs", bufs=6))
+        codes_pool = ctx.enter_context(tc.tile_pool(name="codes", bufs=LOOKAHEAD + 2))
+        out_pool = ctx.enter_context(tc.tile_pool(name="outs", bufs=OUT_BUFS))
         xt_pool = ctx.enter_context(tc.psum_pool(name="xt", bufs=4))
         acc_pool = ctx.enter_context(tc.psum_pool(name="acc", bufs=4))
 
@@ -232,14 +233,15 @@ def tile_hybridsuperlayer_pb_t_kernel(
         w_scales = weights.tile([P, PASSES * D], U8, align_bytes=64)
         nc.vector.quantize_mx(out=w_codes[:].bitcast(FP8X4), scales=w_scales[:], in_=w_grouped[:])
 
-        for c in range(1, RUN):
+        for c in range(1, LOOKAHEAD):
             transpose_chunk(c)
+        for c in range(1, LOOKAHEAD - 1):
             quantise_chunk(c)
 
-        for first in range(0, N_CHUNKS, RUN):
-            for c in range(first + RUN, min(first + 2 * RUN, N_CHUNKS)):
-                transpose_chunk(c)
-            for c in range(first, first + RUN):
-                multiply_chunk(c)
-                if c + RUN < N_CHUNKS:
-                    quantise_chunk(c + RUN)
+        for c in range(N_CHUNKS):
+            ahead = c + LOOKAHEAD
+            if ahead < N_CHUNKS:
+                transpose_chunk(ahead)
+            if 0 < ahead - 1 < N_CHUNKS:
+                quantise_chunk(ahead - 1)
+            multiply_chunk(c)

from contextlib import ExitStack

import concourse.mybir as mybir
from concourse.masks import make_identity

F32 = mybir.dt.float32
BF16 = mybir.dt.bfloat16
U32 = mybir.dt.uint32
U8 = mybir.dt.uint8
FP8X4 = mybir.dt.float8_e4m3fn_x4
MULT = mybir.AluOpType.mult
ADD = mybir.AluOpType.add

P = 128
PACK = 4
TOKENS = 4 * 2048
DFF = 1024
R = 512
D = 512

BANK = 512
PLANES = DFF // P
PASSES = DFF // (P * PACK)
TILES = 4
CHUNK = TILES * P
N_CHUNKS = TOKENS // CHUNK

LOOKAHEAD = 2
H_BUFS = 8
OUT_BUFS = 8

FLOPS = 2 * DFF * R * D + 2 * TOKENS * DFF * D


def tile_hybridsuperlayer_pb_t_kernel(
    tc, h_gelu, c_proj_U, c_proj_S, c_proj_V, c_proj_bias, out
):
    nc = tc.nc
    h_chunks = h_gelu.flatten_outer_dims().rearrange("(c p i) k -> c p (i k)", p=P, i=TILES)
    out_chunks = out.flatten_outer_dims().rearrange("(c p i) d -> c p (i d)", p=P, i=TILES)

    with ExitStack() as ctx:
        ctx.enter_context(tc.manual_schedule())
        const = ctx.enter_context(tc.tile_pool(name="const", bufs=1))
        weights = ctx.enter_context(tc.tile_pool(name="weights", bufs=1))
        h_pool = ctx.enter_context(tc.tile_pool(name="h", bufs=H_BUFS))
        grouped_pool = ctx.enter_context(tc.tile_pool(name="grouped", bufs=3))
        codes_pool = ctx.enter_context(tc.tile_pool(name="codes", bufs=LOOKAHEAD + 2))
        out_pool = ctx.enter_context(tc.tile_pool(name="outs", bufs=OUT_BUFS))
        xt_pool = ctx.enter_context(tc.psum_pool(name="xt", bufs=4))
        acc_pool = ctx.enter_context(tc.psum_pool(name="acc", bufs=4))

        ident = const.tile([P, P], F32)
        make_identity(nc, ident[:])
        ones = const.tile([P, P], BF16)
        nc.vector.memset(ones[:], 1.0)
        bias_rows = const.tile([P, D], BF16)
        nc.vector.memset(bias_rows[:], 0.0)

        s_quad = const.tile([P, PACK], BF16)
        with nc.allow_non_contiguous_dma(reason="512 singular values, two to a piece"):
            nc.sync.dma_start(
                out=s_quad[:].rearrange("q (a b) -> q a b", b=2),
                in_=c_proj_S.rearrange("(a q b) -> q a b", a=2, b=2),
            )

        u_sb = weights.tile([P, PLANES * R], BF16)
        u_view = u_sb[:].rearrange("p (c x) -> p c x", c=4)
        u_dram = c_proj_U.rearrange("(c p e) r -> p c (e r)", c=4, e=2)
        for c in range(4):
            nc.sync.dma_start(out=u_view[:, c, :], in_=u_dram[:, c, :])
        v_sb = weights.tile([P, (D // P) * R], BF16)
        nc.sync.dma_start(
            out=v_sb[:].rearrange("p (t r) -> p t r", r=R),
            in_=c_proj_V.rearrange("(t p) r -> p t r", p=P),
        )
        nc.sync.dma_start(out=bias_rows[0:1, :], in_=c_proj_bias.rearrange("(o d) -> o d", o=1))

        h_tiles = {}

        def load_chunk(c):
            h_sb = h_pool.tile([P, TILES * DFF], BF16)
            nc.sync.dma_start(out=h_sb[:], in_=h_chunks[c])
            h_tiles[c] = h_sb

        for c in range(H_BUFS):
            load_chunk(c)

        u_words = u_sb[:].bitcast(F32)
        us_grouped = weights.tile([P, PLANES * P * PACK], BF16, align_bytes=64)
        s_repeated = (
            s_quad[:].rearrange("q (a b) -> q a b", b=2).unsqueeze(1).to_broadcast([P, 2 * P, 2, 2])
        )
        pair_cols = 2 * P * PACK
        for c in range(PLANES // 2):
            ut = xt_pool.tile([P, BANK], F32, tag="xt")
            for e in range(2):
                for a in range(2):
                    nc.tensor.transpose(
                        ut[:, (2 * a + e) * P : (2 * a + e + 1) * P],
                        u_words[:, (4 * c + 2 * e + a) * P : (4 * c + 2 * e + a + 1) * P],
                        ident[:],
                    )
            nc.vector.tensor_tensor(
                out=us_grouped[:, c * pair_cols : (c + 1) * pair_cols].rearrange(
                    "q (n a b) -> q n a b", a=2, b=2
                ),
                in0=ut[:].bitcast(BF16).rearrange("q (a n b) -> q n a b", a=2, b=2),
                in1=s_repeated,
                op=MULT,
            )

        v_words = v_sb[:].bitcast(F32)
        v_grouped = weights.tile([P, D * PACK], BF16, align_bytes=64)
        v_grouped_words = v_grouped[:].bitcast(F32).rearrange("q (d a) -> q d a", a=2)
        for half in range(2):
            vt = xt_pool.tile([P, BANK], F32, tag="xt")
            for a in range(2):
                for s in range(2):
                    t = 2 * half + s
                    nc.tensor.transpose(
                        vt[:, (2 * a + s) * P : (2 * a + s + 1) * P],
                        v_words[:, (2 * t + a) * P : (2 * t + a + 1) * P],
                        ident[:],
                    )
            nc.scalar.copy(
                out=v_grouped_words[:, half * 256 : (half + 1) * 256, :],
                in_=vt[:].rearrange("q (a d) -> q d a", a=2),
            )

        v_codes = weights.tile([P, D], U32, align_bytes=64)
        v_scales = weights.tile([P, D], U8, align_bytes=64)
        nc.vector.quantize_mx(out=v_codes[:].bitcast(FP8X4), scales=v_scales[:], in_=v_grouped[:])
        us_codes = weights.tile([P, PLANES * P], U32, align_bytes=64)
        us_scales = weights.tile([P, PLANES * P], U8, align_bytes=64)
        for g in range(PASSES):
            nc.vector.quantize_mx(
                out=us_codes[:, g * PACK * P : (g + 1) * PACK * P].bitcast(FP8X4),
                scales=us_scales[:, g * PACK * P : (g + 1) * PACK * P],
                in_=us_grouped[:, g * PACK * P * PACK : (g + 1) * PACK * P * PACK],
            )

        grouped_tiles = {}
        code_tiles = {}

        def transpose_chunk(c):
            h_words = h_tiles[c][:].bitcast(F32)
            grouped = grouped_pool.tile([P, CHUNK * PASSES * PACK], BF16, align_bytes=64)
            grouped_words = grouped[:].bitcast(F32).rearrange(
                "q (i g m u) -> q i g m u", i=TILES, g=PASSES, u=2
            )
            for i in range(TILES):
                xt = xt_pool.tile([P, BANK], F32, tag="xt")
                for w in range(BANK // P):
                    nc.tensor.transpose(
                        xt[:, w * P : (w + 1) * P],
                        h_words[:, (4 * i + w) * P : (4 * i + w + 1) * P],
                        ident[:],
                    )
                nc.scalar.copy(
                    out=grouped_words[:, i],
                    in_=xt[:].rearrange("q (g u m) -> q g m u", g=PASSES, u=2),
                )
            grouped_tiles[c] = grouped
            if c + H_BUFS < N_CHUNKS:
                load_chunk(c + H_BUFS)

        def quantise_chunk(c):
            h_codes = codes_pool.tile([P, CHUNK * PASSES], U32, align_bytes=64)
            h_scales = codes_pool.tile([P, CHUNK * PASSES], U8, align_bytes=64)
            nc.vector.quantize_mx(
                out=h_codes[:].bitcast(FP8X4), scales=h_scales[:], in_=grouped_tiles[c][:]
            )
            code_tiles[c] = (h_codes, h_scales)

        def multiply_chunk(c):
            h_codes, h_scales = code_tiles[c]
            out_sb = out_pool.tile([P, TILES * D], F32)
            for i in range(TILES):
                acc = acc_pool.tile([P, D], F32, tag="acc")
                for g in range(PASSES):
                    tokens = slice((PASSES * i + g) * P, (PASSES * i + g + 1) * P)
                    w_cols = slice(g * D, (g + 1) * D)
                    nc.tensor.matmul_mx(
                        out=acc[:],
                        lhsT=h_codes[:, tokens].bitcast(FP8X4),
                        lhsT_scale=h_scales[:, tokens],
                        rhs=w_codes[:, w_cols].bitcast(FP8X4),
                        rhs_scale=w_scales[:, w_cols],
                        start=(g == 0),
                        stop=(g == PASSES - 1),
                    )
                tile_cols = slice(i * D, (i + 1) * D)
                nc.vector.tensor_tensor(out=out_sb[:, tile_cols], in0=acc[:], in1=bias_bc[:], op=ADD)
                if c == N_CHUNKS - 1:
                    nc.sync.dma_start(out=out_chunks[c][:, tile_cols], in_=out_sb[:, tile_cols])
            if c < N_CHUNKS - 1:
                nc.sync.dma_start(out=out_chunks[c], in_=out_sb[:])

        transpose_chunk(0)

        bias_ps = acc_pool.tile([P, D], F32, tag="acc")
        nc.tensor.matmul(out=bias_ps[:], lhsT=ones[:], rhs=bias_rows[:], start=True, stop=True)
        bias_bc = const.tile([P, D], F32)
        nc.scalar.copy(out=bias_bc[:], in_=bias_ps[:])

        w_grouped = weights.tile([P, PASSES * D * PACK], BF16, align_bytes=64)
        for g in range(PASSES):
            for block in range(D // P):
                w_ps = acc_pool.tile([P, BANK], F32, tag="acc")
                for t in range(PACK):
                    j = PACK * g + t
                    nc.tensor.matmul_mx(
                        out=w_ps[:, t * P : (t + 1) * P],
                        lhsT=us_codes[:, j * P : (j + 1) * P].bitcast(FP8X4),
                        lhsT_scale=us_scales[:, j * P : (j + 1) * P],
                        rhs=v_codes[:, block * P : (block + 1) * P].bitcast(FP8X4),
                        rhs_scale=v_scales[:, block * P : (block + 1) * P],
                        start=True,
                        stop=True,
                    )
                first = (g * (D // P) + block) * BANK
                words_out = w_grouped[:, first : first + BANK].rearrange("p (d t) -> p d t", t=PACK)
                planes_in = w_ps[:].rearrange("p (t d) -> p d t", t=PACK)
                if block % 2 == 0:
                    nc.scalar.copy(out=words_out, in_=planes_in)
                else:
                    nc.vector.tensor_copy(out=words_out, in_=planes_in)

        quantise_chunk(0)

        w_codes = weights.tile([P, PASSES * D], U32, align_bytes=64)
        w_scales = weights.tile([P, PASSES * D], U8, align_bytes=64)
        nc.vector.quantize_mx(out=w_codes[:].bitcast(FP8X4), scales=w_scales[:], in_=w_grouped[:])

        for c in range(1, LOOKAHEAD):
            transpose_chunk(c)
        for c in range(1, LOOKAHEAD - 1):
            quantise_chunk(c)

        for c in range(N_CHUNKS):
            ahead = c + LOOKAHEAD
            if ahead < N_CHUNKS:
                transpose_chunk(ahead)
            if 0 < ahead - 1 < N_CHUNKS:
                quantise_chunk(ahead - 1)
            multiply_chunk(c)
